import numpy as np
import ml_dtypes


def mxq(x, axis, fmt="e4m3"):
    dtype, down = {"e4m3": (ml_dtypes.float8_e4m3fn, 7), "e5m2": (ml_dtypes.float8_e5m2, 14)}[fmt]
    v = np.moveaxis(np.asarray(x, np.float32).astype(ml_dtypes.bfloat16).astype(np.float64), axis, -1)
    blocks = v.reshape(v.shape[:-1] + (-1, 32))
    amax = np.abs(blocks).max(-1, keepdims=True)
    byte = np.maximum(np.where(amax > 0, np.frexp(amax)[1] - 1 + 127, 0) - down, 1)
    scale = np.exp2(byte - 127.0)
    codes = (blocks / scale).astype(np.float32).astype(dtype).astype(np.float64)
    return np.moveaxis((codes * scale).reshape(v.shape), -1, axis)


WIDE = False


def mx_kscale(k):
    if not WIDE:
        return np.ones(k)
    levels = np.array([10, -10, 5, -5, 0])
    a = np.random.permutation(np.resize(levels, k // 512 * 4)).reshape(k // 512, 4)
    idx = np.arange(k)
    return np.exp2(a[idx // 512, idx % 128 // 32])


BF16 = ml_dtypes.bfloat16


def bf(x):
    return np.asarray(x, np.float32).astype(BF16)


def f64(x):
    return np.asarray(x).astype(np.float64)


B, N, ATTR, STATE, REL, G, NF = 32, 4, 4, 16, 9, 32, 512


def setup_inputs():
    rn = np.random.standard_normal
    s, u, t = mx_kscale(NF), mx_kscale(NF), mx_kscale(NF)
    rp_rows = np.concatenate([s, u, u])
    pp_rows = np.concatenate([u, t])
    pp_scale = np.concatenate([np.full(NF, 1.0 / np.sqrt(NF)), np.full(NF, 1.0 / np.sqrt(NF * N))])
    return {
        "rel_enc": bf(np.maximum(rn((B, N, N, NF)) * 1.1, 0.0) * s),
        "obj": bf(np.maximum(rn((B, N, NF)) * 1.1, 0.0) * u),
        "rp_w": bf(rn((3 * NF, NF)) * 2.0 / np.sqrt(3 * NF * N) / rp_rows[:, None] * t),
        "rp_b": bf(rn(NF) * 0.1 * t),
        "pp_w": bf(rn((2 * NF, NF)) * (pp_scale / pp_rows)[:, None]),
        "pp_b": bf(rn(NF) * 0.1),
    }


def reference(rel_enc, obj, rp_w, rp_b, pp_w, pp_b):
    rp, pp = f64(rp_w), f64(pp_w)
    oq = mxq(f64(obj), 2, "e4m3")
    e_rel = mxq(f64(rel_enc), 3, "e4m3") @ mxq(rp[:NF], 0, "e4m3")
    e_recv = oq @ mxq(rp[NF:2 * NF], 0, "e4m3")
    e_send = oq @ mxq(rp[2 * NF:], 0, "e4m3")
    rel_eff = np.maximum(e_rel + e_recv[:, :, None, :] + e_send[:, None, :, :] + f64(rp_b), 0.0)
    agg = rel_eff.sum(axis=2)
    p_obj = oq @ mxq(pp[:NF], 0, "e4m3")
    p_agg = mxq(agg, 2, "e4m3") @ mxq(pp[NF:], 0, "e4m3")
    return np.maximum(p_obj + p_agg + f64(pp_b), 0.0)

@@ -1,0 +1,193 @@
+from contextlib import ExitStack
+
+import concourse.mybir as mybir
+from concourse.masks import make_identity
+
+F32 = mybir.dt.float32
+BF16 = mybir.dt.bfloat16
+U32 = mybir.dt.uint32
+U8 = mybir.dt.uint8
+FP8X4 = mybir.dt.float8_e4m3fn_x4
+RELU = mybir.ActivationFunctionType.Relu
+
+P = 128
+PACK = 4
+NF = 512
+BATCH = 32
+NPART = 4
+ROWS = BATCH * NPART
+RELS = ROWS * NPART
+HALF = NF // 2
+RUN = 4
+
+FLOPS = 2 * NF * NF * (RELS + 4 * ROWS)
+
+
+def tile_compositionalkoopmanoperators_pa_s_kernel(tc, rel_enc, obj, rp_w, rp_b, pp_w, pp_b, out):
+    nc = tc.nc
+    with ExitStack() as ctx:
+        keep = ctx.enter_context(tc.tile_pool(name="keep", bufs=1))
+        work = ctx.enter_context(tc.tile_pool(name="work", bufs=2))
+        psum = ctx.enter_context(tc.psum_pool(name="psum", bufs=1))
+
+        obj_sb = keep.tile([P, NF], BF16)
+        nc.sync.dma_start(out=obj_sb[:], in_=obj.rearrange("b i f -> (b i) f"))
+        rel_sb = keep.tile([P, NPART * NF], BF16)
+        nc.sync.dma_start(out=rel_sb[:], in_=rel_enc.rearrange("b i j f -> (b i) (j f)"))
+
+        rp_bias = keep.tile([P, PACK], BF16)
+        with nc.allow_non_contiguous_dma(reason="512 bias values, one element a piece"):
+            nc.scalar.dma_start(out=rp_bias[:], in_=rp_b.rearrange("(t p) -> p t", t=PACK, p=P))
+
+        def load_pair_order(name, rows):
+            raw = keep.tile([P, PACK, NF], BF16, name=name)
+            nc.sync.dma_start(
+                out=raw[:].rearrange("p (u e) n -> p u (e n)", u=2),
+                in_=rows.rearrange("(u p e) n -> p u (e n)", u=2, p=P, e=2),
+            )
+            return raw
+
+        def load_plane_order(name, rows):
+            raw = keep.tile([P, PACK, NF], BF16, name=name)
+            nc.sync.dma_start(out=raw[:], in_=rows.rearrange("(t p) n -> p t n", t=PACK, p=P))
+            return raw
+
+        raw_rel = load_pair_order("raw_rel", rp_w[0:NF, :])
+        raw_recv = load_pair_order("raw_recv", rp_w[NF : 2 * NF, :])
+        raw_send = load_pair_order("raw_send", rp_w[2 * NF : 3 * NF, :])
+        raw_pobj = load_pair_order("raw_pobj", pp_w[0:NF, :])
+        raw_pagg = load_plane_order("raw_pagg", pp_w[NF : 2 * NF, :])
+
+        pp_bias = keep.tile([P, NF], BF16)
+        nc.sync.dma_start(out=pp_bias[:], in_=pp_b.partition_broadcast(P))
+
+        ident = keep.tile([P, P], F32)
+        make_identity(nc, ident[:])
+
+        obj_words = obj_sb[:].bitcast(F32)
+        obj_t = psum.tile([P, 2, ROWS], F32, tag="obj_t")
+        for u in range(2):
+            nc.tensor.transpose(obj_t[:, u, :], obj_words[:, u * P : (u + 1) * P], ident[:])
+
+        rel_words = rel_sb[:].bitcast(F32)
+        rel_t = []
+        for h in range(2):
+            bank = psum.tile([P, 2, 2, ROWS], F32, tag="half%d" % h, name="rel_t%d" % h)
+            for jj in range(2):
+                for u in range(2):
+                    first = ((2 * h + jj) * 2 + u) * P
+                    nc.tensor.transpose(bank[:, jj, u, :], rel_words[:, first : first + P], ident[:])
+            rel_t.append(bank)
+
+        obj_grouped = keep.tile([P, ROWS * PACK], BF16, align_bytes=64)
+        nc.scalar.copy(
+            out=obj_grouped[:].bitcast(F32).rearrange("p (r u) -> p r u", u=2),
+            in_=obj_t[:].rearrange("p u r -> p r u"),
+        )
+        send_grouped = keep.tile([P, RELS * PACK], BF16, align_bytes=64)
+        send_view = send_grouped[:].bitcast(F32).rearrange("p (j b i u) -> p j b i u", j=NPART, b=BATCH, i=NPART)
+        obj_by_sender = obj_t[:].rearrange("p u (b j) -> p j b u", j=NPART)
+        for j in range(NPART):
+            nc.scalar.copy(
+                out=send_view[:, j],
+                in_=obj_by_sender[:, j].unsqueeze(2).to_broadcast([P, BATCH, NPART, 2]),
+            )
+        rel_grouped = keep.tile([P, RELS * PACK], BF16, align_bytes=64)
+        rel_view = rel_grouped[:].bitcast(F32).rearrange("p (h jj r u) -> p h jj r u", h=2, jj=2, u=2)
+        for h in range(2):
+            nc.vector.tensor_copy(out=rel_view[:, h], in_=rel_t[h][:].rearrange("p jj u r -> p jj r u"))
+
+        recv_codes = keep.tile([P, RELS], U32, align_bytes=64)
+        recv_scales = keep.tile([P, RELS], U8, align_bytes=64)
+        for j in range(NPART):
+            cols = slice(j * ROWS, (j + 1) * ROWS)
+            nc.vector.quantize_mx(out=recv_codes[:, cols].bitcast(FP8X4), scales=recv_scales[:, cols], in_=obj_grouped[:])
+        send_codes = keep.tile([P, RELS], U32, align_bytes=64)
+        send_scales = keep.tile([P, RELS], U8, align_bytes=64)
+        nc.vector.quantize_mx(out=send_codes[:].bitcast(FP8X4), scales=send_scales[:], in_=send_grouped[:])
+        rel_codes = keep.tile([P, RELS], U32, align_bytes=64)
+        rel_scales = keep.tile([P, RELS], U8, align_bytes=64)
+        nc.vector.quantize_mx(out=rel_codes[:].bitcast(FP8X4), scales=rel_scales[:], in_=rel_grouped[:])
+
+        def quantise_weight(name, raw):
+            grouped = keep.tile([P, NF, PACK], BF16, name=name + "_grouped", align_bytes=64)
+            codes = keep.tile([P, NF], U32, name=name + "_codes", align_bytes=64)
+            scales = keep.tile([P, NF], U8, name=name + "_scales", align_bytes=64)
+            for h, copy in enumerate((nc.vector.tensor_copy, nc.scalar.copy)):
+                cols = slice(h * HALF, (h + 1) * HALF)
+                copy(
+                    out=grouped[:, cols, :].rearrange("p (c i) t -> p c t i", i=RUN),
+                    in_=raw[:, :, cols].rearrange("p t (c i) -> p c t i", i=RUN),
+                )
+            for h in range(2):
+                cols = slice(h * HALF, (h + 1) * HALF)
+                nc.vector.quantize_mx(
+                    out=codes[:, cols].bitcast(FP8X4),
+                    scales=scales[:, cols],
+                    in_=grouped[:, cols, :].rearrange("p n t -> p (n t)"),
+                )
+            return codes, scales
+
+        acc = [psum.tile([P, RELS], F32, tag="acc%d" % m, name="acc%d" % m) for m in range(PACK)]
+        stage1 = (
+            ("w_rel", raw_rel, rel_codes, rel_scales),
+            ("w_recv", raw_recv, recv_codes, recv_scales),
+            ("w_send", raw_send, send_codes, send_scales),
+        )
+        for step, (name, raw, x_codes, x_scales) in enumerate(stage1):
+            w_codes, w_scales = quantise_weight(name, raw)
+            for m in range(PACK):
+                cols = slice(m * P, (m + 1) * P)
+                nc.tensor.matmul_mx(
+                    out=acc[m][:],
+                    lhsT=w_codes[:, cols].bitcast(FP8X4),
+                    lhsT_scale=w_scales[:, cols],
+                    rhs=x_codes[:].bitcast(FP8X4),
+                    rhs_scale=x_scales[:],
+                    start=(step == 0),
+                    stop=(step == len(stage1) - 1),
+                )
+
+        agg_grouped = keep.tile([P, ROWS, PACK], BF16, align_bytes=64)
+        for m in range(PACK):
+            eff = work.tile([P, NPART, ROWS], F32)
+            nc.scalar.activation(
+                out=eff[:].rearrange("p j r -> p (j r)"), in_=acc[m][:], func=RELU, bias=rp_bias[:, m : m + 1], scale=1.0
+            )
+            pair = work.tile([P, 2, ROWS], F32)
+            nc.vector.tensor_add(out=pair[:], in0=eff[:, 0:2, :], in1=eff[:, 2:4, :])
+            nc.vector.tensor_add(out=agg_grouped[:, :, m], in0=pair[:, 0, :], in1=pair[:, 1, :])
+        agg_codes = keep.tile([P, ROWS], U32, align_bytes=64)
+        agg_scales = keep.tile([P, ROWS], U8, align_bytes=64)
+        nc.vector.quantize_mx(
+            out=agg_codes[:].bitcast(FP8X4), scales=agg_scales[:], in_=agg_grouped[:].rearrange("p r t -> p (r t)")
+        )
+
+        pobj_codes, pobj_scales = quantise_weight("p_obj", raw_pobj)
+        pagg_codes, pagg_scales = quantise_weight("p_agg", raw_pagg)
+        out_rows = out.rearrange("b i f -> (b i) f")
+        result = keep.tile([P, NF], F32)
+        for h in range(2):
+            cols = slice(h * HALF, (h + 1) * HALF)
+            out_ps = psum.tile([P, HALF], F32, tag="half%d" % h, name="out_ps%d" % h)
+            nc.tensor.matmul_mx(
+                out=out_ps[:],
+                lhsT=recv_codes[:, 0:ROWS].bitcast(FP8X4),
+                lhsT_scale=recv_scales[:, 0:ROWS],
+                rhs=pobj_codes[:, cols].bitcast(FP8X4),
+                rhs_scale=pobj_scales[:, cols],
+                start=True,
+                stop=False,
+            )
+            nc.tensor.matmul_mx(
+                out=out_ps[:],
+                lhsT=agg_codes[:].bitcast(FP8X4),
+                lhsT_scale=agg_scales[:],
+                rhs=pagg_codes[:, cols].bitcast(FP8X4),
+                rhs_scale=pagg_scales[:, cols],
+                start=False,
+                stop=True,
+            )
+            nc.vector.tensor_add(out=result[:, cols], in0=out_ps[:], in1=pp_bias[:, cols])
+            nc.scalar.activation(out=result[:, cols], in_=result[:, cols], func=RELU)
+            nc.sync.dma_start(out=out_rows[:, cols], in_=result[:, cols])

@@ -20,14 +20,17 @@ RELS = ROWS * NPART
 HALF = NF // 2
 RUN = 4
 
+VECTOR_COLS_STAGE1 = 256
+VECTOR_COLS_STAGE2 = 128
+
 FLOPS = 2 * NF * NF * (RELS + 4 * ROWS)
 
 
 def tile_compositionalkoopmanoperators_pa_s_kernel(tc, rel_enc, obj, rp_w, rp_b, pp_w, pp_b, out):
     nc = tc.nc
     with ExitStack() as ctx:
+        ctx.enter_context(tc.manual_schedule())
         keep = ctx.enter_context(tc.tile_pool(name="keep", bufs=1))
-        work = ctx.enter_context(tc.tile_pool(name="work", bufs=2))
         psum = ctx.enter_context(tc.psum_pool(name="psum", bufs=1))
 
         obj_sb = keep.tile([P, NF], BF16)
@@ -64,6 +67,36 @@ def tile_compositionalkoopmanoperators_pa_s_kernel(tc, rel_enc, obj, rp_w, rp_b,
         ident = keep.tile([P, P], F32)
         make_identity(nc, ident[:])
 
+        def regroup(copy, grouped, raw, first, last):
+            copy(
+                out=grouped[:, first:last, :].rearrange("p (c i) t -> p c t i", i=RUN),
+                in_=raw[:, :, first:last].rearrange("p t (c i) -> p c t i", i=RUN),
+            )
+
+        def regroup_weight(name, raw, vector_cols):
+            grouped = keep.tile([P, NF, PACK], BF16, name=name + "_grouped", align_bytes=64)
+            regroup(nc.vector.tensor_copy, grouped, raw, 0, vector_cols)
+            regroup(nc.scalar.copy, grouped, raw, vector_cols, NF)
+            return grouped
+
+        def quantise_weight(name, grouped):
+            codes = keep.tile([P, NF], U32, name=name + "_codes", align_bytes=64)
+            scales = keep.tile([P, NF], U8, name=name + "_scales", align_bytes=64)
+            for h in range(2):
+                cols = slice(h * HALF, (h + 1) * HALF)
+                nc.vector.quantize_mx(
+                    out=codes[:, cols].bitcast(FP8X4),
+                    scales=scales[:, cols],
+                    in_=grouped[:, cols, :].rearrange("p n t -> p (n t)"),
+                )
+            return codes, scales
+
+        def quantise_activation(name, grouped):
+            codes = keep.tile([P, RELS], U32, name=name + "_codes", align_bytes=64)
+            scales = keep.tile([P, RELS], U8, name=name + "_scales", align_bytes=64)
+            nc.vector.quantize_mx(out=codes[:].bitcast(FP8X4), scales=scales[:], in_=grouped[:])
+            return codes, scales
+
         obj_words = obj_sb[:].bitcast(F32)
         obj_t = psum.tile([P, 2, ROWS], F32, tag="obj_t")
         for u in range(2):
@@ -84,6 +117,11 @@ def tile_compositionalkoopmanoperators_pa_s_kernel(tc, rel_enc, obj, rp_w, rp_b,
             out=obj_grouped[:].bitcast(F32).rearrange("p (r u) -> p r u", u=2),
             in_=obj_t[:].rearrange("p u r -> p r u"),
         )
+        recv_codes = keep.tile([P, RELS], U32, align_bytes=64)
+        recv_scales = keep.tile([P, RELS], U8, align_bytes=64)
+        for j in range(NPART):
+            cols = slice(j * ROWS, (j + 1) * ROWS)
+            nc.vector.quantize_mx(out=recv_codes[:, cols].bitcast(FP8X4), scales=recv_scales[:, cols], in_=obj_grouped[:])
         send_grouped = keep.tile([P, RELS * PACK], BF16, align_bytes=64)
         send_view = send_grouped[:].bitcast(F32).rearrange("p (j b i u) -> p j b i u", j=NPART, b=BATCH, i=NPART)
         obj_by_sender = obj_t[:].rearrange("p u (b j) -> p j b u", j=NPART)
@@ -94,48 +132,12 @@ def tile_compositionalkoopmanoperators_pa_s_kernel(tc, rel_enc, obj, rp_w, rp_b,
             )
         rel_grouped = keep.tile([P, RELS * PACK], BF16, align_bytes=64)
         rel_view = rel_grouped[:].bitcast(F32).rearrange("p (h jj r u) -> p h jj r u", h=2, jj=2, u=2)
-        for h in range(2):
-            nc.vector.tensor_copy(out=rel_view[:, h], in_=rel_t[h][:].rearrange("p jj u r -> p jj r u"))
-
-        recv_codes = keep.tile([P, RELS], U32, align_bytes=64)
-        recv_scales = keep.tile([P, RELS], U8, align_bytes=64)
-        for j in range(NPART):
-            cols = slice(j * ROWS, (j + 1) * ROWS)
-            nc.vector.quantize_mx(out=recv_codes[:, cols].bitcast(FP8X4), scales=recv_scales[:, cols], in_=obj_grouped[:])
-        send_codes = keep.tile([P, RELS], U32, align_bytes=64)
-        send_scales = keep.tile([P, RELS], U8, align_bytes=64)
-        nc.vector.quantize_mx(out=send_codes[:].bitcast(FP8X4), scales=send_scales[:], in_=send_grouped[:])
-        rel_codes = keep.tile([P, RELS], U32, align_bytes=64)
-        rel_scales = keep.tile([P, RELS], U8, align_bytes=64)
-        nc.vector.quantize_mx(out=rel_codes[:].bitcast(FP8X4), scales=rel_scales[:], in_=rel_grouped[:])
-
-        def quantise_weight(name, raw):
-            grouped = keep.tile([P, NF, PACK], BF16, name=name + "_grouped", align_bytes=64)
-            codes = keep.tile([P, NF], U32, name=name + "_codes", align_bytes=64)
-            scales = keep.tile([P, NF], U8, name=name + "_scales", align_bytes=64)
-            for h, copy in enumerate((nc.vector.tensor_copy, nc.scalar.copy)):
-                cols = slice(h * HALF, (h + 1) * HALF)
-                copy(
-                    out=grouped[:, cols, :].rearrange("p (c i) t -> p c t i", i=RUN),
-                    in_=raw[:, :, cols].rearrange("p t (c i) -> p c t i", i=RUN),
-                )
-            for h in range(2):
-                cols = slice(h * HALF, (h + 1) * HALF)
-                nc.vector.quantize_mx(
-                    out=codes[:, cols].bitcast(FP8X4),
-                    scales=scales[:, cols],
-                    in_=grouped[:, cols, :].rearrange("p n t -> p (n t)"),
-                )
-            return codes, scales
+        for h, copy in enumerate((nc.vector.tensor_copy, nc.scalar.copy)):
+            copy(out=rel_view[:, h], in_=rel_t[h][:].rearrange("p jj u r -> p jj r u"))
 
         acc = [psum.tile([P, RELS], F32, tag="acc%d" % m, name="acc%d" % m) for m in range(PACK)]
-        stage1 = (
-            ("w_rel", raw_rel, rel_codes, rel_scales),
-            ("w_recv", raw_recv, recv_codes, recv_scales),
-            ("w_send", raw_send, send_codes, send_scales),
-        )
-        for step, (name, raw, x_codes, x_scales) in enumerate(stage1):
-            w_codes, w_scales = quantise_weight(name, raw)
+
+        def first_stage_passes(w_codes, w_scales, x_codes, x_scales, start, stop):
             for m in range(PACK):
                 cols = slice(m * P, (m + 1) * P)
                 nc.tensor.matmul_mx(
@@ -144,17 +146,36 @@ def tile_compositionalkoopmanoperators_pa_s_kernel(tc, rel_enc, obj, rp_w, rp_b,
                     lhsT_scale=w_scales[:, cols],
                     rhs=x_codes[:].bitcast(FP8X4),
                     rhs_scale=x_scales[:],
-                    start=(step == 0),
-                    stop=(step == len(stage1) - 1),
+                    start=start,
+                    stop=stop,
                 )
+
+        grouped = regroup_weight("w_rel", raw_rel, VECTOR_COLS_STAGE1)
+        rel_codes, rel_scales = quantise_activation("rel", rel_grouped)
+        w_codes, w_scales = quantise_weight("w_rel", grouped)
+        first_stage_passes(w_codes, w_scales, rel_codes, rel_scales, True, False)
+
+        grouped = regroup_weight("w_recv", raw_recv, VECTOR_COLS_STAGE1)
+        send_codes, send_scales = quantise_activation("send", send_grouped)
+        w_codes, w_scales = quantise_weight("w_recv", grouped)
+        first_stage_passes(w_codes, w_scales, recv_codes, recv_scales, False, False)
+
+        grouped = regroup_weight("w_send", raw_send, VECTOR_COLS_STAGE1)
+        w_codes, w_scales = quantise_weight("w_send", grouped)
+        first_stage_passes(w_codes, w_scales, send_codes, send_scales, False, True)
+
+        pobj_grouped = regroup_weight("p_obj", raw_pobj, VECTOR_COLS_STAGE2)
+        pagg_grouped = keep.tile([P, NF, PACK], BF16, align_bytes=64)
+        regroup(nc.vector.tensor_copy, pagg_grouped, raw_pagg, 0, VECTOR_COLS_STAGE2)
+        pobj_codes, pobj_scales = quantise_weight("p_obj", pobj_grouped)
 
         agg_grouped = keep.tile([P, ROWS, PACK], BF16, align_bytes=64)
         for m in range(PACK):
-            eff = work.tile([P, NPART, ROWS], F32)
+            eff = keep.tile([P, NPART, ROWS], F32, name="eff%d" % m)
             nc.scalar.activation(
                 out=eff[:].rearrange("p j r -> p (j r)"), in_=acc[m][:], func=RELU, bias=rp_bias[:, m : m + 1], scale=1.0
             )
-            pair = work.tile([P, 2, ROWS], F32)
+            pair = keep.tile([P, 2, ROWS], F32, name="pair%d" % m)
             nc.vector.tensor_add(out=pair[:], in0=eff[:, 0:2, :], in1=eff[:, 2:4, :])
             nc.vector.tensor_add(out=agg_grouped[:, :, m], in0=pair[:, 0, :], in1=pair[:, 1, :])
         agg_codes = keep.tile([P, ROWS], U32, align_bytes=64)
@@ -163,15 +184,15 @@ def tile_compositionalkoopmanoperators_pa_s_kernel(tc, rel_enc, obj, rp_w, rp_b,
             out=agg_codes[:].bitcast(FP8X4), scales=agg_scales[:], in_=agg_grouped[:].rearrange("p r t -> p (r t)")
         )
 
-        pobj_codes, pobj_scales = quantise_weight("p_obj", raw_pobj)
-        pagg_codes, pagg_scales = quantise_weight("p_agg", raw_pagg)
+        regroup(nc.scalar.copy, pagg_grouped, raw_pagg, VECTOR_COLS_STAGE2, NF)
+        pagg_codes, pagg_scales = quantise_weight("p_agg", pagg_grouped)
+
         out_rows = out.rearrange("b i f -> (b i) f")
-        result = keep.tile([P, NF], F32)
+        out_ps = [psum.tile([P, HALF], F32, tag="half%d" % h, name="out_ps%d" % h) for h in range(2)]
         for h in range(2):
             cols = slice(h * HALF, (h + 1) * HALF)
-            out_ps = psum.tile([P, HALF], F32, tag="half%d" % h, name="out_ps%d" % h)
             nc.tensor.matmul_mx(
-                out=out_ps[:],
+                out=out_ps[h][:],
                 lhsT=recv_codes[:, 0:ROWS].bitcast(FP8X4),
                 lhsT_scale=recv_scales[:, 0:ROWS],
                 rhs=pobj_codes[:, cols].bitcast(FP8X4),
@@ -179,8 +200,11 @@ def tile_compositionalkoopmanoperators_pa_s_kernel(tc, rel_enc, obj, rp_w, rp_b,
                 start=True,
                 stop=False,
             )
+        result = keep.tile([P, NF], F32)
+        for h in range(2):
+            cols = slice(h * HALF, (h + 1) * HALF)
             nc.tensor.matmul_mx(
-                out=out_ps[:],
+                out=out_ps[h][:],
                 lhsT=agg_codes[:].bitcast(FP8X4),
                 lhsT_scale=agg_scales[:],
                 rhs=pagg_codes[:, cols].bitcast(FP8X4),
@@ -188,6 +212,6 @@ def tile_compositionalkoopmanoperators_pa_s_kernel(tc, rel_enc, obj, rp_w, rp_b,
                 start=False,
                 stop=True,
             )
-            nc.vector.tensor_add(out=result[:, cols], in0=out_ps[:], in1=pp_bias[:, cols])
+            nc.vector.tensor_add(out=result[:, cols], in0=out_ps[h][:], in1=pp_bias[:, cols])
             nc.scalar.activation(out=result[:, cols], in_=result[:, cols], func=RELU)
             nc.sync.dma_start(out=out_rows[:, cols], in_=result[:, cols])

@@ -18,10 +18,8 @@ NPART = 4
 ROWS = BATCH * NPART
 RELS = ROWS * NPART
 HALF = NF // 2
+LOW, HIGH = 0, 1
 RUN = 4
-
-VECTOR_COLS_STAGE1 = 256
-VECTOR_COLS_STAGE2 = 128
 
 FLOPS = 2 * NF * NF * (RELS + 4 * ROWS)
 
@@ -35,31 +33,43 @@ def tile_compositionalkoopmanoperators_pa_s_kernel(tc, rel_enc, obj, rp_w, rp_b,
 
         obj_sb = keep.tile([P, NF], BF16)
         nc.sync.dma_start(out=obj_sb[:], in_=obj.rearrange("b i f -> (b i) f"))
-        rel_sb = keep.tile([P, NPART * NF], BF16)
-        nc.sync.dma_start(out=rel_sb[:], in_=rel_enc.rearrange("b i j f -> (b i) (j f)"))
+        rel_rows = rel_enc.rearrange("b i (h jj) f -> h (b i) (jj f)", h=2)
+        rel_sb = []
+        for h in range(2):
+            rel_half = keep.tile([P, 2 * NF], BF16, name="rel_sb%d" % h)
+            nc.sync.dma_start(out=rel_half[:], in_=rel_rows[h])
+            rel_sb.append(rel_half)
 
         rp_bias = keep.tile([P, PACK], BF16)
         with nc.allow_non_contiguous_dma(reason="512 bias values, one element a piece"):
-            nc.scalar.dma_start(out=rp_bias[:], in_=rp_b.rearrange("(t p) -> p t", t=PACK, p=P))
+            nc.scalar.dma_start(out=rp_bias[:], in_=rp_b.rearrange("(m p) -> p m", m=PACK, p=P))
+
+        def weight_tiles(name):
+            return {
+                "raw": keep.tile([P, PACK, NF], BF16, name=name + "_raw"),
+                "grouped": keep.tile([P, NF, PACK], BF16, name=name + "_grouped", align_bytes=64),
+                "codes": keep.tile([P, NF], U32, name=name + "_codes", align_bytes=64),
+                "scales": keep.tile([P, NF], U8, name=name + "_scales", align_bytes=64),
+            }
 
         def load_pair_order(name, rows):
-            raw = keep.tile([P, PACK, NF], BF16, name=name)
+            w = weight_tiles(name)
             nc.sync.dma_start(
-                out=raw[:].rearrange("p (u e) n -> p u (e n)", u=2),
+                out=w["raw"][:].rearrange("p (u e) n -> p u (e n)", u=2),
                 in_=rows.rearrange("(u p e) n -> p u (e n)", u=2, p=P, e=2),
             )
-            return raw
+            return w
 
         def load_plane_order(name, rows):
-            raw = keep.tile([P, PACK, NF], BF16, name=name)
-            nc.sync.dma_start(out=raw[:], in_=rows.rearrange("(t p) n -> p t n", t=PACK, p=P))
-            return raw
+            w = weight_tiles(name)
+            nc.sync.dma_start(out=w["raw"][:], in_=rows.rearrange("(t p) n -> p t n", t=PACK, p=P))
+            return w
 
-        raw_rel = load_pair_order("raw_rel", rp_w[0:NF, :])
-        raw_recv = load_pair_order("raw_recv", rp_w[NF : 2 * NF, :])
-        raw_send = load_pair_order("raw_send", rp_w[2 * NF : 3 * NF, :])
-        raw_pobj = load_pair_order("raw_pobj", pp_w[0:NF, :])
-        raw_pagg = load_plane_order("raw_pagg", pp_w[NF : 2 * NF, :])
+        w_rel = load_pair_order("w_rel", rp_w[0:NF, :])
+        w_recv = load_pair_order("w_recv", rp_w[NF : 2 * NF, :])
+        w_send = load_pair_order("w_send", rp_w[2 * NF : 3 * NF, :])
+        p_obj = load_pair_order("p_obj", pp_w[0:NF, :])
+        p_agg = load_plane_order("p_agg", pp_w[NF : 2 * NF, :])
 
         pp_bias = keep.tile([P, NF], BF16)
         nc.sync.dma_start(out=pp_bias[:], in_=pp_b.partition_broadcast(P))
@@ -67,48 +77,32 @@ def tile_compositionalkoopmanoperators_pa_s_kernel(tc, rel_enc, obj, rp_w, rp_b,
         ident = keep.tile([P, P], F32)
         make_identity(nc, ident[:])
 
-        def regroup(copy, grouped, raw, first, last):
+        def regroup_half(copy, w, h):
+            cols = slice(h * HALF, (h + 1) * HALF)
             copy(
-                out=grouped[:, first:last, :].rearrange("p (c i) t -> p c t i", i=RUN),
-                in_=raw[:, :, first:last].rearrange("p t (c i) -> p c t i", i=RUN),
+                out=w["grouped"][:, cols, :].rearrange("p (c i) t -> p c t i", i=RUN),
+                in_=w["raw"][:, :, cols].rearrange("p t (c i) -> p c t i", i=RUN),
             )
 
-        def regroup_weight(name, raw, vector_cols):
-            grouped = keep.tile([P, NF, PACK], BF16, name=name + "_grouped", align_bytes=64)
-            regroup(nc.vector.tensor_copy, grouped, raw, 0, vector_cols)
-            regroup(nc.scalar.copy, grouped, raw, vector_cols, NF)
-            return grouped
-
-        def quantise_weight(name, grouped):
-            codes = keep.tile([P, NF], U32, name=name + "_codes", align_bytes=64)
-            scales = keep.tile([P, NF], U8, name=name + "_scales", align_bytes=64)
-            for h in range(2):
-                cols = slice(h * HALF, (h + 1) * HALF)
-                nc.vector.quantize_mx(
-                    out=codes[:, cols].bitcast(FP8X4),
-                    scales=scales[:, cols],
-                    in_=grouped[:, cols, :].rearrange("p n t -> p (n t)"),
-                )
-            return codes, scales
-
-        def quantise_activation(name, grouped):
-            codes = keep.tile([P, RELS], U32, name=name + "_codes", align_bytes=64)
-            scales = keep.tile([P, RELS], U8, name=name + "_scales", align_bytes=64)
-            nc.vector.quantize_mx(out=codes[:].bitcast(FP8X4), scales=scales[:], in_=grouped[:])
-            return codes, scales
+        def quantise_half(w, h):
+            cols = slice(h * HALF, (h + 1) * HALF)
+            nc.vector.quantize_mx(
+                out=w["codes"][:, cols].bitcast(FP8X4),
+                scales=w["scales"][:, cols],
+                in_=w["grouped"][:, cols, :].rearrange("p n t -> p (n t)"),
+            )
 
         obj_words = obj_sb[:].bitcast(F32)
         obj_t = psum.tile([P, 2, ROWS], F32, tag="obj_t")
         for u in range(2):
             nc.tensor.transpose(obj_t[:, u, :], obj_words[:, u * P : (u + 1) * P], ident[:])
-
-        rel_words = rel_sb[:].bitcast(F32)
         rel_t = []
         for h in range(2):
+            rel_words = rel_sb[h][:].bitcast(F32)
             bank = psum.tile([P, 2, 2, ROWS], F32, tag="half%d" % h, name="rel_t%d" % h)
             for jj in range(2):
                 for u in range(2):
-                    first = ((2 * h + jj) * 2 + u) * P
+                    first = (jj * 2 + u) * P
                     nc.tensor.transpose(bank[:, jj, u, :], rel_words[:, first : first + P], ident[:])
             rel_t.append(bank)
 
@@ -117,11 +111,9 @@ def tile_compositionalkoopmanoperators_pa_s_kernel(tc, rel_enc, obj, rp_w, rp_b,
             out=obj_grouped[:].bitcast(F32).rearrange("p (r u) -> p r u", u=2),
             in_=obj_t[:].rearrange("p u r -> p r u"),
         )
-        recv_codes = keep.tile([P, RELS], U32, align_bytes=64)
-        recv_scales = keep.tile([P, RELS], U8, align_bytes=64)
-        for j in range(NPART):
-            cols = slice(j * ROWS, (j + 1) * ROWS)
-            nc.vector.quantize_mx(out=recv_codes[:, cols].bitcast(FP8X4), scales=recv_scales[:, cols], in_=obj_grouped[:])
+        obj_codes = keep.tile([P, ROWS], U32, align_bytes=64)
+        obj_scales = keep.tile([P, ROWS], U8, align_bytes=64)
+        nc.vector.quantize_mx(out=obj_codes[:].bitcast(FP8X4), scales=obj_scales[:], in_=obj_grouped[:])
         send_grouped = keep.tile([P, RELS * PACK], BF16, align_bytes=64)
         send_view = send_grouped[:].bitcast(F32).rearrange("p (j b i u) -> p j b i u", j=NPART, b=BATCH, i=NPART)
         obj_by_sender = obj_t[:].rearrange("p u (b j) -> p j b u", j=NPART)
@@ -134,84 +126,112 @@ def tile_compositionalkoopmanoperators_pa_s_kernel(tc, rel_enc, obj, rp_w, rp_b,
         rel_view = rel_grouped[:].bitcast(F32).rearrange("p (h jj r u) -> p h jj r u", h=2, jj=2, u=2)
         for h, copy in enumerate((nc.vector.tensor_copy, nc.scalar.copy)):
             copy(out=rel_view[:, h], in_=rel_t[h][:].rearrange("p jj u r -> p jj r u"))
+        rel_codes = keep.tile([P, RELS], U32, align_bytes=64)
+        rel_scales = keep.tile([P, RELS], U8, align_bytes=64)
+        send_codes = keep.tile([P, RELS], U32, align_bytes=64)
+        send_scales = keep.tile([P, RELS], U8, align_bytes=64)
 
         acc = [psum.tile([P, RELS], F32, tag="acc%d" % m, name="acc%d" % m) for m in range(PACK)]
 
-        def first_stage_passes(w_codes, w_scales, x_codes, x_scales, start, stop):
-            for m in range(PACK):
-                cols = slice(m * P, (m + 1) * P)
-                nc.tensor.matmul_mx(
-                    out=acc[m][:],
-                    lhsT=w_codes[:, cols].bitcast(FP8X4),
-                    lhsT_scale=w_scales[:, cols],
-                    rhs=x_codes[:].bitcast(FP8X4),
-                    rhs_scale=x_scales[:],
-                    start=start,
-                    stop=stop,
-                )
+        def first_stage_pass(w, m, out_cols, x_codes, x_scales, start, stop):
+            cols = slice(m * P, (m + 1) * P)
+            nc.tensor.matmul_mx(
+                out=out_cols,
+                lhsT=w["codes"][:, cols].bitcast(FP8X4),
+                lhsT_scale=w["scales"][:, cols],
+                rhs=x_codes[:].bitcast(FP8X4),
+                rhs_scale=x_scales[:],
+                start=start,
+                stop=stop,
+            )
 
-        grouped = regroup_weight("w_rel", raw_rel, VECTOR_COLS_STAGE1)
-        rel_codes, rel_scales = quantise_activation("rel", rel_grouped)
-        w_codes, w_scales = quantise_weight("w_rel", grouped)
-        first_stage_passes(w_codes, w_scales, rel_codes, rel_scales, True, False)
+        def relation_passes(h):
+            for m in (2 * h, 2 * h + 1):
+                first_stage_pass(w_rel, m, acc[m][:], rel_codes, rel_scales, True, False)
 
-        grouped = regroup_weight("w_recv", raw_recv, VECTOR_COLS_STAGE1)
-        send_codes, send_scales = quantise_activation("send", send_grouped)
-        w_codes, w_scales = quantise_weight("w_recv", grouped)
-        first_stage_passes(w_codes, w_scales, recv_codes, recv_scales, False, False)
+        def receiver_passes(h):
+            for m in (2 * h, 2 * h + 1):
+                by_sender = acc[m][:].rearrange("p (j r) -> p j r", j=NPART)
+                for j in range(NPART):
+                    first_stage_pass(w_recv, m, by_sender[:, j], obj_codes, obj_scales, False, False)
 
-        grouped = regroup_weight("w_send", raw_send, VECTOR_COLS_STAGE1)
-        w_codes, w_scales = quantise_weight("w_send", grouped)
-        first_stage_passes(w_codes, w_scales, send_codes, send_scales, False, True)
+        def sender_passes(h):
+            for m in (2 * h, 2 * h + 1):
+                first_stage_pass(w_send, m, acc[m][:], send_codes, send_scales, False, True)
 
-        pobj_grouped = regroup_weight("p_obj", raw_pobj, VECTOR_COLS_STAGE2)
-        pagg_grouped = keep.tile([P, NF, PACK], BF16, align_bytes=64)
-        regroup(nc.vector.tensor_copy, pagg_grouped, raw_pagg, 0, VECTOR_COLS_STAGE2)
-        pobj_codes, pobj_scales = quantise_weight("p_obj", pobj_grouped)
+        out_ps = [psum.tile([P, HALF], F32, tag="half%d" % h, name="out_ps%d" % h) for h in range(2)]
+
+        def second_stage_pass(w, h, x_codes, x_scales, start, stop):
+            cols = slice(h * HALF, (h + 1) * HALF)
+            nc.tensor.matmul_mx(
+                out=out_ps[h][:],
+                lhsT=x_codes[:].bitcast(FP8X4),
+                lhsT_scale=x_scales[:],
+                rhs=w["codes"][:, cols].bitcast(FP8X4),
+                rhs_scale=w["scales"][:, cols],
+                start=start,
+                stop=stop,
+            )
+
+        regroup_half(nc.vector.tensor_copy, w_rel, LOW)
+        regroup_half(nc.scalar.copy, w_rel, HIGH)
+        nc.vector.quantize_mx(out=rel_codes[:].bitcast(FP8X4), scales=rel_scales[:], in_=rel_grouped[:])
+        quantise_half(w_rel, LOW)
+        relation_passes(LOW)
+        nc.vector.quantize_mx(out=send_codes[:].bitcast(FP8X4), scales=send_scales[:], in_=send_grouped[:])
+
+        regroup_half(nc.vector.tensor_copy, w_recv, LOW)
+        regroup_half(nc.scalar.copy, w_recv, HIGH)
+        quantise_half(w_rel, HIGH)
+        relation_passes(HIGH)
+        quantise_half(w_recv, LOW)
+        receiver_passes(LOW)
+
+        regroup_half(nc.vector.tensor_copy, w_send, LOW)
+        regroup_half(nc.scalar.copy, w_send, HIGH)
+        quantise_half(w_recv, HIGH)
+        receiver_passes(HIGH)
+        quantise_half(w_send, LOW)
+        sender_passes(LOW)
+
+        regroup_half(nc.vector.tensor_copy, p_obj, LOW)
+        regroup_half(nc.scalar.copy, p_obj, HIGH)
+        quantise_half(w_send, HIGH)
+        sender_passes(HIGH)
+        quantise_half(p_obj, LOW)
+        second_stage_pass(p_obj, LOW, obj_codes, obj_scales, True, False)
+
+        regroup_half(nc.vector.tensor_copy, p_agg, LOW)
+        quantise_half(p_obj, HIGH)
+        second_stage_pass(p_obj, HIGH, obj_codes, obj_scales, True, False)
+        quantise_half(p_agg, LOW)
 
         agg_grouped = keep.tile([P, ROWS, PACK], BF16, align_bytes=64)
+        eff = [keep.tile([P, NPART, ROWS], F32, name="eff%d" % m) for m in range(PACK)]
+        pair = [keep.tile([P, 2, ROWS], F32, name="pair%d" % m) for m in range(PACK)]
         for m in range(PACK):
-            eff = keep.tile([P, NPART, ROWS], F32, name="eff%d" % m)
             nc.scalar.activation(
-                out=eff[:].rearrange("p j r -> p (j r)"), in_=acc[m][:], func=RELU, bias=rp_bias[:, m : m + 1], scale=1.0
+                out=eff[m][:].rearrange("p j r -> p (j r)"), in_=acc[m][:], func=RELU, bias=rp_bias[:, m : m + 1], scale=1.0
             )
-            pair = keep.tile([P, 2, ROWS], F32, name="pair%d" % m)
-            nc.vector.tensor_add(out=pair[:], in0=eff[:, 0:2, :], in1=eff[:, 2:4, :])
-            nc.vector.tensor_add(out=agg_grouped[:, :, m], in0=pair[:, 0, :], in1=pair[:, 1, :])
+        for h in range(2):
+            for m in (2 * h, 2 * h + 1):
+                nc.vector.tensor_add(out=pair[m][:], in0=eff[m][:, 0:2, :], in1=eff[m][:, 2:4, :])
+            for m in (2 * h, 2 * h + 1):
+                nc.vector.tensor_add(out=agg_grouped[:, :, m], in0=pair[m][:, 0, :], in1=pair[m][:, 1, :])
+
+        regroup_half(nc.scalar.copy, p_agg, HIGH)
+        quantise_half(p_agg, HIGH)
         agg_codes = keep.tile([P, ROWS], U32, align_bytes=64)
         agg_scales = keep.tile([P, ROWS], U8, align_bytes=64)
         nc.vector.quantize_mx(
             out=agg_codes[:].bitcast(FP8X4), scales=agg_scales[:], in_=agg_grouped[:].rearrange("p r t -> p (r t)")
         )
 
-        regroup(nc.scalar.copy, pagg_grouped, raw_pagg, VECTOR_COLS_STAGE2, NF)
-        pagg_codes, pagg_scales = quantise_weight("p_agg", pagg_grouped)
-
         out_rows = out.rearrange("b i f -> (b i) f")
-        out_ps = [psum.tile([P, HALF], F32, tag="half%d" % h, name="out_ps%d" % h) for h in range(2)]
-        for h in range(2):
-            cols = slice(h * HALF, (h + 1) * HALF)
-            nc.tensor.matmul_mx(
-                out=out_ps[h][:],
-                lhsT=recv_codes[:, 0:ROWS].bitcast(FP8X4),
-                lhsT_scale=recv_scales[:, 0:ROWS],
-                rhs=pobj_codes[:, cols].bitcast(FP8X4),
-                rhs_scale=pobj_scales[:, cols],
-                start=True,
-                stop=False,
-            )
         result = keep.tile([P, NF], F32)
         for h in range(2):
             cols = slice(h * HALF, (h + 1) * HALF)
-            nc.tensor.matmul_mx(
-                out=out_ps[h][:],
-                lhsT=agg_codes[:].bitcast(FP8X4),
-                lhsT_scale=agg_scales[:],
-                rhs=pagg_codes[:, cols].bitcast(FP8X4),
-                rhs_scale=pagg_scales[:, cols],
-                start=False,
-                stop=True,
-            )
+            second_stage_pass(p_agg, h, agg_codes, agg_scales, False, True)
             nc.vector.tensor_add(out=result[:, cols], in0=out_ps[h][:], in1=pp_bias[:, cols])
             nc.scalar.activation(out=result[:, cols], in_=result[:, cols], func=RELU)
             nc.sync.dma_start(out=out_rows[:, cols], in_=result[:, cols])

@@ -9,6 +9,8 @@ U32 = mybir.dt.uint32
 U8 = mybir.dt.uint8
 FP8X4 = mybir.dt.float8_e4m3fn_x4
 RELU = mybir.ActivationFunctionType.Relu
+ADD = mybir.AluOpType.add
+MAX = mybir.AluOpType.max
 
 P = 128
 PACK = 4
@@ -20,6 +22,9 @@ RELS = ROWS * NPART
 HALF = NF // 2
 LOW, HIGH = 0, 1
 RUN = 4
+
+VECTOR_COLS_STAGE1 = 256
+VECTOR_COLS_STAGE2 = 128
 
 FLOPS = 2 * NF * NF * (RELS + 4 * ROWS)
 
@@ -39,10 +44,6 @@ def tile_compositionalkoopmanoperators_pa_s_kernel(tc, rel_enc, obj, rp_w, rp_b,
             rel_half = keep.tile([P, 2 * NF], BF16, name="rel_sb%d" % h)
             nc.sync.dma_start(out=rel_half[:], in_=rel_rows[h])
             rel_sb.append(rel_half)
-
-        rp_bias = keep.tile([P, PACK], BF16)
-        with nc.allow_non_contiguous_dma(reason="512 bias values, one element a piece"):
-            nc.scalar.dma_start(out=rp_bias[:], in_=rp_b.rearrange("(m p) -> p m", m=PACK, p=P))
 
         def weight_tiles(name):
             return {
@@ -71,18 +72,26 @@ def tile_compositionalkoopmanoperators_pa_s_kernel(tc, rel_enc, obj, rp_w, rp_b,
         p_obj = load_pair_order("p_obj", pp_w[0:NF, :])
         p_agg = load_plane_order("p_agg", pp_w[NF : 2 * NF, :])
 
+        rp_bias = keep.tile([P, PACK], BF16)
+        with nc.allow_non_contiguous_dma(reason="512 bias values, one element a piece"):
+            nc.sync.dma_start(out=rp_bias[:], in_=rp_b.rearrange("(m p) -> p m", m=PACK, p=P))
         pp_bias = keep.tile([P, NF], BF16)
         nc.sync.dma_start(out=pp_bias[:], in_=pp_b.partition_broadcast(P))
 
         ident = keep.tile([P, P], F32)
         make_identity(nc, ident[:])
 
-        def regroup_half(copy, w, h):
-            cols = slice(h * HALF, (h + 1) * HALF)
+        def regroup(copy, grouped, raw, first, last):
             copy(
-                out=w["grouped"][:, cols, :].rearrange("p (c i) t -> p c t i", i=RUN),
-                in_=w["raw"][:, :, cols].rearrange("p t (c i) -> p c t i", i=RUN),
+                out=grouped[:, first:last, :].rearrange("p (c i) t -> p c t i", i=RUN),
+                in_=raw[:, :, first:last].rearrange("p t (c i) -> p c t i", i=RUN),
             )
+
+        def regroup_on_vector(w, vector_cols):
+            regroup(nc.vector.tensor_copy, w["grouped"], w["raw"], 0, vector_cols)
+
+        def regroup_on_scalar(w, vector_cols):
+            regroup(nc.scalar.copy, w["grouped"], w["raw"], vector_cols, NF)
 
         def quantise_half(w, h):
             cols = slice(h * HALF, (h + 1) * HALF)
@@ -173,56 +182,74 @@ def tile_compositionalkoopmanoperators_pa_s_kernel(tc, rel_enc, obj, rp_w, rp_b,
                 stop=stop,
             )
 
-        regroup_half(nc.vector.tensor_copy, w_rel, LOW)
-        regroup_half(nc.scalar.copy, w_rel, HIGH)
+        regroup_on_vector(w_rel, VECTOR_COLS_STAGE1)
+        regroup_on_scalar(w_rel, VECTOR_COLS_STAGE1)
         nc.vector.quantize_mx(out=rel_codes[:].bitcast(FP8X4), scales=rel_scales[:], in_=rel_grouped[:])
         quantise_half(w_rel, LOW)
         relation_passes(LOW)
         nc.vector.quantize_mx(out=send_codes[:].bitcast(FP8X4), scales=send_scales[:], in_=send_grouped[:])
 
-        regroup_half(nc.vector.tensor_copy, w_recv, LOW)
-        regroup_half(nc.scalar.copy, w_recv, HIGH)
+        regroup_on_vector(w_recv, VECTOR_COLS_STAGE1)
+        regroup_on_scalar(w_recv, VECTOR_COLS_STAGE1)
         quantise_half(w_rel, HIGH)
         relation_passes(HIGH)
         quantise_half(w_recv, LOW)
         receiver_passes(LOW)
 
-        regroup_half(nc.vector.tensor_copy, w_send, LOW)
-        regroup_half(nc.scalar.copy, w_send, HIGH)
+        regroup_on_vector(w_send, VECTOR_COLS_STAGE1)
+        regroup_on_scalar(w_send, VECTOR_COLS_STAGE1)
         quantise_half(w_recv, HIGH)
         receiver_passes(HIGH)
         quantise_half(w_send, LOW)
         sender_passes(LOW)
 
-        regroup_half(nc.vector.tensor_copy, p_obj, LOW)
-        regroup_half(nc.scalar.copy, p_obj, HIGH)
+        regroup_on_vector(p_obj, VECTOR_COLS_STAGE2)
+        regroup_on_scalar(p_obj, VECTOR_COLS_STAGE2)
         quantise_half(w_send, HIGH)
         sender_passes(HIGH)
-        quantise_half(p_obj, LOW)
-        second_stage_pass(p_obj, LOW, obj_codes, obj_scales, True, False)
+        regroup_on_vector(p_agg, VECTOR_COLS_STAGE2)
+        for h in (LOW, HIGH):
+            quantise_half(p_obj, h)
+            second_stage_pass(p_obj, h, obj_codes, obj_scales, True, False)
 
-        regroup_half(nc.vector.tensor_copy, p_agg, LOW)
-        quantise_half(p_obj, HIGH)
-        second_stage_pass(p_obj, HIGH, obj_codes, obj_scales, True, False)
-        quantise_half(p_agg, LOW)
-
-        agg_grouped = keep.tile([P, ROWS, PACK], BF16, align_bytes=64)
-        eff = [keep.tile([P, NPART, ROWS], F32, name="eff%d" % m) for m in range(PACK)]
+        minus_bias = keep.tile([P, PACK], F32)
+        nc.vector.tensor_scalar_mul(out=minus_bias[:], in0=rp_bias[:], scalar1=-1.0)
+        twice_bias = keep.tile([P, PACK], F32)
+        nc.vector.tensor_scalar_mul(out=twice_bias[:], in0=rp_bias[:], scalar1=2.0)
+        eff = [keep.tile([P, 2 * ROWS], F32, name="eff%d" % m) for m in range(PACK)]
         pair = [keep.tile([P, 2, ROWS], F32, name="pair%d" % m) for m in range(PACK)]
+        agg_planes = keep.tile([P, PACK, ROWS], BF16)
         for m in range(PACK):
             nc.scalar.activation(
-                out=eff[m][:].rearrange("p j r -> p (j r)"), in_=acc[m][:], func=RELU, bias=rp_bias[:, m : m + 1], scale=1.0
+                out=eff[m][:], in_=acc[m][:, 0 : 2 * ROWS], func=RELU, bias=rp_bias[:, m : m + 1], scale=1.0
             )
         for h in range(2):
             for m in (2 * h, 2 * h + 1):
-                nc.vector.tensor_add(out=pair[m][:], in0=eff[m][:, 0:2, :], in1=eff[m][:, 2:4, :])
+                nc.vector.scalar_tensor_tensor(
+                    out=pair[m][:].rearrange("p j r -> p (j r)"),
+                    in0=acc[m][:, 2 * ROWS : RELS],
+                    scalar=minus_bias[:, m : m + 1],
+                    in1=eff[m][:],
+                    op0=MAX,
+                    op1=ADD,
+                )
             for m in (2 * h, 2 * h + 1):
-                nc.vector.tensor_add(out=agg_grouped[:, :, m], in0=pair[m][:, 0, :], in1=pair[m][:, 1, :])
+                nc.vector.scalar_tensor_tensor(
+                    out=agg_planes[:, m, :],
+                    in0=pair[m][:, 0, :],
+                    scalar=twice_bias[:, m : m + 1],
+                    in1=pair[m][:, 1, :],
+                    op0=ADD,
+                    op1=ADD,
+                )
 
-        regroup_half(nc.scalar.copy, p_agg, HIGH)
-        quantise_half(p_agg, HIGH)
+        regroup_on_scalar(p_agg, VECTOR_COLS_STAGE2)
+        agg_grouped = keep.tile([P, ROWS, PACK], BF16, align_bytes=64)
         agg_codes = keep.tile([P, ROWS], U32, align_bytes=64)
         agg_scales = keep.tile([P, ROWS], U8, align_bytes=64)
+        quantise_half(p_agg, LOW)
+        regroup(nc.vector.tensor_copy, agg_grouped, agg_planes, 0, ROWS)
+        quantise_half(p_agg, HIGH)
         nc.vector.quantize_mx(
             out=agg_codes[:].bitcast(FP8X4), scales=agg_scales[:], in_=agg_grouped[:].rearrange("p r t -> p (r t)")
         )

@@ -247,12 +247,12 @@ def tile_compositionalkoopmanoperators_pa_s_kernel(tc, rel_enc, obj, rp_w, rp_b,
         agg_grouped = keep.tile([P, ROWS, PACK], BF16, align_bytes=64)
         agg_codes = keep.tile([P, ROWS], U32, align_bytes=64)
         agg_scales = keep.tile([P, ROWS], U8, align_bytes=64)
-        quantise_half(p_agg, LOW)
         regroup(nc.vector.tensor_copy, agg_grouped, agg_planes, 0, ROWS)
-        quantise_half(p_agg, HIGH)
+        quantise_half(p_agg, LOW)
         nc.vector.quantize_mx(
             out=agg_codes[:].bitcast(FP8X4), scales=agg_scales[:], in_=agg_grouped[:].rearrange("p r t -> p (r t)")
         )
+        quantise_half(p_agg, HIGH)
 
         out_rows = out.rearrange("b i f -> (b i) f")
         result = keep.tile([P, NF], F32)

@@ -70,16 +70,21 @@ def tile_compositionalkoopmanoperators_pa_s_kernel(tc, rel_enc, obj, rp_w, rp_b,
         w_recv = load_pair_order("w_recv", rp_w[NF : 2 * NF, :])
         w_send = load_pair_order("w_send", rp_w[2 * NF : 3 * NF, :])
         p_obj = load_pair_order("p_obj", pp_w[0:NF, :])
-        p_agg = load_plane_order("p_agg", pp_w[NF : 2 * NF, :])
-
         rp_bias = keep.tile([P, PACK], BF16)
         with nc.allow_non_contiguous_dma(reason="512 bias values, one element a piece"):
             nc.sync.dma_start(out=rp_bias[:], in_=rp_b.rearrange("(m p) -> p m", m=PACK, p=P))
+        p_agg = load_plane_order("p_agg", pp_w[NF : 2 * NF, :])
+
         pp_bias = keep.tile([P, NF], BF16)
         nc.sync.dma_start(out=pp_bias[:], in_=pp_b.partition_broadcast(P))
 
         ident = keep.tile([P, P], F32)
         make_identity(nc, ident[:])
+
+        minus_bias = keep.tile([P, PACK], F32)
+        nc.gpsimd.tensor_scalar_mul(out=minus_bias[:], in0=rp_bias[:], scalar1=-1.0)
+        twice_bias = keep.tile([P, PACK], F32)
+        nc.gpsimd.tensor_scalar_mul(out=twice_bias[:], in0=rp_bias[:], scalar1=2.0)
 
         def regroup(copy, grouped, raw, first, last):
             copy(
@@ -212,10 +217,6 @@ def tile_compositionalkoopmanoperators_pa_s_kernel(tc, rel_enc, obj, rp_w, rp_b,
             quantise_half(p_obj, h)
             second_stage_pass(p_obj, h, obj_codes, obj_scales, True, False)
 
-        minus_bias = keep.tile([P, PACK], F32)
-        nc.vector.tensor_scalar_mul(out=minus_bias[:], in0=rp_bias[:], scalar1=-1.0)
-        twice_bias = keep.tile([P, PACK], F32)
-        nc.vector.tensor_scalar_mul(out=twice_bias[:], in0=rp_bias[:], scalar1=2.0)
         eff = [keep.tile([P, 2 * ROWS], F32, name="eff%d" % m) for m in range(PACK)]
         pair = [keep.tile([P, 2, ROWS], F32, name="pair%d" % m) for m in range(PACK)]
         agg_planes = keep.tile([P, PACK, ROWS], BF16)

@@ -26,6 +26,8 @@ RUN = 4
 VECTOR_COLS_STAGE1 = 256
 VECTOR_COLS_STAGE2 = 128
 
+WARM_PASSES = 14
+
 FLOPS = 2 * NF * NF * (RELS + 4 * ROWS)
 
 
@@ -144,6 +146,18 @@ def tile_compositionalkoopmanoperators_pa_s_kernel(tc, rel_enc, obj, rp_w, rp_b,
         rel_scales = keep.tile([P, RELS], U8, align_bytes=64)
         send_codes = keep.tile([P, RELS], U32, align_bytes=64)
         send_scales = keep.tile([P, RELS], U8, align_bytes=64)
+
+        warm = psum.tile([P, ROWS], F32, tag="warm")
+        for repeat in range(WARM_PASSES):
+            nc.tensor.matmul_mx(
+                out=warm[:],
+                lhsT=obj_codes[:].bitcast(FP8X4),
+                lhsT_scale=obj_scales[:],
+                rhs=obj_codes[:].bitcast(FP8X4),
+                rhs_scale=obj_scales[:],
+                start=True,
+                stop=True,
+            )
 
         acc = [psum.tile([P, RELS], F32, tag="acc%d" % m, name="acc%d" % m) for m in range(PACK)]
 

@@ -24,9 +24,10 @@ LOW, HIGH = 0, 1
 RUN = 4
 
 VECTOR_COLS_STAGE1 = 256
-VECTOR_COLS_STAGE2 = 128
+VECTOR_COLS_P_OBJ = 256
+VECTOR_COLS_P_AGG = 128
 
-WARM_PASSES = 14
+WARM_PASSES = 8
 
 FLOPS = 2 * NF * NF * (RELS + 4 * ROWS)
 
@@ -40,13 +41,6 @@ def tile_compositionalkoopmanoperators_pa_s_kernel(tc, rel_enc, obj, rp_w, rp_b,
 
         obj_sb = keep.tile([P, NF], BF16)
         nc.sync.dma_start(out=obj_sb[:], in_=obj.rearrange("b i f -> (b i) f"))
-        rel_rows = rel_enc.rearrange("b i (h jj) f -> h (b i) (jj f)", h=2)
-        rel_sb = []
-        for h in range(2):
-            rel_half = keep.tile([P, 2 * NF], BF16, name="rel_sb%d" % h)
-            nc.sync.dma_start(out=rel_half[:], in_=rel_rows[h])
-            rel_sb.append(rel_half)
-
         def weight_tiles(name):
             return {
                 "raw": keep.tile([P, PACK, NF], BF16, name=name + "_raw"),
@@ -69,6 +63,13 @@ def tile_compositionalkoopmanoperators_pa_s_kernel(tc, rel_enc, obj, rp_w, rp_b,
             return w
 
         w_rel = load_pair_order("w_rel", rp_w[0:NF, :])
+        rel_rows = rel_enc.rearrange("b i (h jj) f -> h (b i) (jj f)", h=2)
+        rel_sb = []
+        for h in range(2):
+            rel_half = keep.tile([P, 2 * NF], BF16, name="rel_sb%d" % h)
+            nc.sync.dma_start(out=rel_half[:], in_=rel_rows[h])
+            rel_sb.append(rel_half)
+
         w_recv = load_pair_order("w_recv", rp_w[NF : 2 * NF, :])
         w_send = load_pair_order("w_send", rp_w[2 * NF : 3 * NF, :])
         p_obj = load_pair_order("p_obj", pp_w[0:NF, :])
@@ -109,9 +110,12 @@ def tile_compositionalkoopmanoperators_pa_s_kernel(tc, rel_enc, obj, rp_w, rp_b,
             )
 
         obj_words = obj_sb[:].bitcast(F32)
-        obj_t = psum.tile([P, 2, ROWS], F32, tag="obj_t")
-        for u in range(2):
-            nc.tensor.transpose(obj_t[:, u, :], obj_words[:, u * P : (u + 1) * P], ident[:])
+        obj_t = []
+        for reader in ("vector", "scalar"):
+            bank = psum.tile([P, 2, ROWS], F32, tag="obj_" + reader, name="obj_t_" + reader)
+            for u in range(2):
+                nc.tensor.transpose(bank[:, u, :], obj_words[:, u * P : (u + 1) * P], ident[:])
+            obj_t.append(bank)
         rel_t = []
         for h in range(2):
             rel_words = rel_sb[h][:].bitcast(F32)
@@ -123,31 +127,34 @@ def tile_compositionalkoopmanoperators_pa_s_kernel(tc, rel_enc, obj, rp_w, rp_b,
             rel_t.append(bank)
 
         obj_grouped = keep.tile([P, ROWS * PACK], BF16, align_bytes=64)
-        nc.scalar.copy(
+        nc.vector.tensor_copy(
             out=obj_grouped[:].bitcast(F32).rearrange("p (r u) -> p r u", u=2),
-            in_=obj_t[:].rearrange("p u r -> p r u"),
+            in_=obj_t[0][:].rearrange("p u r -> p r u"),
         )
         obj_codes = keep.tile([P, ROWS], U32, align_bytes=64)
         obj_scales = keep.tile([P, ROWS], U8, align_bytes=64)
-        nc.vector.quantize_mx(out=obj_codes[:].bitcast(FP8X4), scales=obj_scales[:], in_=obj_grouped[:])
         send_grouped = keep.tile([P, RELS * PACK], BF16, align_bytes=64)
         send_view = send_grouped[:].bitcast(F32).rearrange("p (j b i u) -> p j b i u", j=NPART, b=BATCH, i=NPART)
-        obj_by_sender = obj_t[:].rearrange("p u (b j) -> p j b u", j=NPART)
         for j in range(NPART):
-            nc.scalar.copy(
+            copy, bank = (nc.vector.tensor_copy, obj_t[0]) if j == 0 else (nc.scalar.copy, obj_t[1])
+            obj_by_sender = bank[:].rearrange("p u (b j) -> p j b u", j=NPART)
+            copy(
                 out=send_view[:, j],
                 in_=obj_by_sender[:, j].unsqueeze(2).to_broadcast([P, BATCH, NPART, 2]),
             )
+        nc.vector.quantize_mx(out=obj_codes[:].bitcast(FP8X4), scales=obj_scales[:], in_=obj_grouped[:])
+        regroup_on_vector(w_rel, VECTOR_COLS_STAGE1)
+        regroup_on_scalar(w_rel, VECTOR_COLS_STAGE1)
         rel_grouped = keep.tile([P, RELS * PACK], BF16, align_bytes=64)
         rel_view = rel_grouped[:].bitcast(F32).rearrange("p (h jj r u) -> p h jj r u", h=2, jj=2, u=2)
-        for h, copy in enumerate((nc.vector.tensor_copy, nc.scalar.copy)):
-            copy(out=rel_view[:, h], in_=rel_t[h][:].rearrange("p jj u r -> p jj r u"))
+        for h in range(2):
+            nc.scalar.copy(out=rel_view[:, h], in_=rel_t[h][:].rearrange("p jj u r -> p jj r u"))
         rel_codes = keep.tile([P, RELS], U32, align_bytes=64)
         rel_scales = keep.tile([P, RELS], U8, align_bytes=64)
         send_codes = keep.tile([P, RELS], U32, align_bytes=64)
         send_scales = keep.tile([P, RELS], U8, align_bytes=64)
 
-        warm = psum.tile([P, ROWS], F32, tag="warm")
+        warm = psum.tile([P, ROWS], F32, tag="obj_vector", name="warm")
         for repeat in range(WARM_PASSES):
             nc.tensor.matmul_mx(
                 out=warm[:],
@@ -167,25 +174,34 @@ def tile_compositionalkoopmanoperators_pa_s_kernel(tc, rel_enc, obj, rp_w, rp_b,
                 out=out_cols,
                 lhsT=w["codes"][:, cols].bitcast(FP8X4),
                 lhsT_scale=w["scales"][:, cols],
-                rhs=x_codes[:].bitcast(FP8X4),
-                rhs_scale=x_scales[:],
+                rhs=x_codes.bitcast(FP8X4),
+                rhs_scale=x_scales,
                 start=start,
                 stop=stop,
             )
 
+        def quantise_relations(h):
+            cols = slice(h * RELS // 2, (h + 1) * RELS // 2)
+            nc.vector.quantize_mx(
+                out=rel_codes[:, cols].bitcast(FP8X4),
+                scales=rel_scales[:, cols],
+                in_=rel_grouped[:, h * RELS // 2 * PACK : (h + 1) * RELS // 2 * PACK],
+            )
+
         def relation_passes(h):
-            for m in (2 * h, 2 * h + 1):
-                first_stage_pass(w_rel, m, acc[m][:], rel_codes, rel_scales, True, False)
+            cols = slice(h * RELS // 2, (h + 1) * RELS // 2)
+            for m in range(PACK):
+                first_stage_pass(w_rel, m, acc[m][:, cols], rel_codes[:, cols], rel_scales[:, cols], h == 0, False)
 
         def receiver_passes(h):
             for m in (2 * h, 2 * h + 1):
                 by_sender = acc[m][:].rearrange("p (j r) -> p j r", j=NPART)
                 for j in range(NPART):
-                    first_stage_pass(w_recv, m, by_sender[:, j], obj_codes, obj_scales, False, False)
+                    first_stage_pass(w_recv, m, by_sender[:, j], obj_codes[:], obj_scales[:], False, False)
 
         def sender_passes(h):
             for m in (2 * h, 2 * h + 1):
-                first_stage_pass(w_send, m, acc[m][:], send_codes, send_scales, False, True)
+                first_stage_pass(w_send, m, acc[m][:], send_codes[:], send_scales[:], False, True)
 
         out_ps = [psum.tile([P, HALF], F32, tag="half%d" % h, name="out_ps%d" % h) for h in range(2)]
 
@@ -201,35 +217,30 @@ def tile_compositionalkoopmanoperators_pa_s_kernel(tc, rel_enc, obj, rp_w, rp_b,
                 stop=stop,
             )
 
-        regroup_on_vector(w_rel, VECTOR_COLS_STAGE1)
-        regroup_on_scalar(w_rel, VECTOR_COLS_STAGE1)
-        nc.vector.quantize_mx(out=rel_codes[:].bitcast(FP8X4), scales=rel_scales[:], in_=rel_grouped[:])
-        quantise_half(w_rel, LOW)
-        relation_passes(LOW)
         nc.vector.quantize_mx(out=send_codes[:].bitcast(FP8X4), scales=send_scales[:], in_=send_grouped[:])
-
+        quantise_half(w_rel, LOW)
+        quantise_half(w_rel, HIGH)
+        quantise_relations(0)
+        relation_passes(0)
         regroup_on_vector(w_recv, VECTOR_COLS_STAGE1)
         regroup_on_scalar(w_recv, VECTOR_COLS_STAGE1)
-        quantise_half(w_rel, HIGH)
-        relation_passes(HIGH)
+        quantise_relations(1)
+        relation_passes(1)
         quantise_half(w_recv, LOW)
         receiver_passes(LOW)
-
         regroup_on_vector(w_send, VECTOR_COLS_STAGE1)
         regroup_on_scalar(w_send, VECTOR_COLS_STAGE1)
         quantise_half(w_recv, HIGH)
         receiver_passes(HIGH)
         quantise_half(w_send, LOW)
         sender_passes(LOW)
-
-        regroup_on_vector(p_obj, VECTOR_COLS_STAGE2)
-        regroup_on_scalar(p_obj, VECTOR_COLS_STAGE2)
         quantise_half(w_send, HIGH)
         sender_passes(HIGH)
-        regroup_on_vector(p_agg, VECTOR_COLS_STAGE2)
-        for h in (LOW, HIGH):
-            quantise_half(p_obj, h)
-            second_stage_pass(p_obj, h, obj_codes, obj_scales, True, False)
+        regroup_on_vector(p_obj, VECTOR_COLS_P_OBJ)
+        regroup_on_scalar(p_obj, VECTOR_COLS_P_OBJ)
+        regroup_on_vector(p_agg, VECTOR_COLS_P_AGG)
+        quantise_half(p_obj, LOW)
+        second_stage_pass(p_obj, LOW, obj_codes, obj_scales, True, False)
 
         eff = [keep.tile([P, 2 * ROWS], F32, name="eff%d" % m) for m in range(PACK)]
         pair = [keep.tile([P, 2, ROWS], F32, name="pair%d" % m) for m in range(PACK)]
@@ -258,10 +269,12 @@ def tile_compositionalkoopmanoperators_pa_s_kernel(tc, rel_enc, obj, rp_w, rp_b,
                     op1=ADD,
                 )
 
-        regroup_on_scalar(p_agg, VECTOR_COLS_STAGE2)
+        regroup_on_scalar(p_agg, VECTOR_COLS_P_AGG)
         agg_grouped = keep.tile([P, ROWS, PACK], BF16, align_bytes=64)
         agg_codes = keep.tile([P, ROWS], U32, align_bytes=64)
         agg_scales = keep.tile([P, ROWS], U8, align_bytes=64)
+        quantise_half(p_obj, HIGH)
+        second_stage_pass(p_obj, HIGH, obj_codes, obj_scales, True, False)
         regroup(nc.vector.tensor_copy, agg_grouped, agg_planes, 0, ROWS)
         quantise_half(p_agg, LOW)
         nc.vector.quantize_mx(

@@ -21,13 +21,15 @@ ROWS = BATCH * NPART
 RELS = ROWS * NPART
 HALF = NF // 2
 LOW, HIGH = 0, 1
+PIECES = ((0, 256), (256, 384), (384, 512))
 RUN = 4
 
+VECTOR_COLS_W_REL = 320
 VECTOR_COLS_STAGE1 = 256
 VECTOR_COLS_P_OBJ = 256
-VECTOR_COLS_P_AGG = 128
 
 WARM_PASSES = 8
+STAY_WARM_PASSES = 4
 
 FLOPS = 2 * NF * NF * (RELS + 4 * ROWS)
 
@@ -83,6 +85,8 @@ def tile_compositionalkoopmanoperators_pa_s_kernel(tc, rel_enc, obj, rp_w, rp_b,
 
         ident = keep.tile([P, P], F32)
         make_identity(nc, ident[:])
+        ident_bf16 = keep.tile([P, P], BF16)
+        make_identity(nc, ident_bf16[:])
 
         minus_bias = keep.tile([P, PACK], F32)
         nc.gpsimd.tensor_scalar_mul(out=minus_bias[:], in0=rp_bias[:], scalar1=-1.0)
@@ -143,8 +147,8 @@ def tile_compositionalkoopmanoperators_pa_s_kernel(tc, rel_enc, obj, rp_w, rp_b,
                 in_=obj_by_sender[:, j].unsqueeze(2).to_broadcast([P, BATCH, NPART, 2]),
             )
         nc.vector.quantize_mx(out=obj_codes[:].bitcast(FP8X4), scales=obj_scales[:], in_=obj_grouped[:])
-        regroup_on_vector(w_rel, VECTOR_COLS_STAGE1)
-        regroup_on_scalar(w_rel, VECTOR_COLS_STAGE1)
+        regroup_on_vector(w_rel, VECTOR_COLS_W_REL)
+        regroup_on_scalar(w_rel, VECTOR_COLS_W_REL)
         rel_grouped = keep.tile([P, RELS * PACK], BF16, align_bytes=64)
         rel_view = rel_grouped[:].bitcast(F32).rearrange("p (h jj r u) -> p h jj r u", h=2, jj=2, u=2)
         for h in range(2):
@@ -203,12 +207,10 @@ def tile_compositionalkoopmanoperators_pa_s_kernel(tc, rel_enc, obj, rp_w, rp_b,
             for m in (2 * h, 2 * h + 1):
                 first_stage_pass(w_send, m, acc[m][:], send_codes[:], send_scales[:], False, True)
 
-        out_ps = [psum.tile([P, HALF], F32, tag="half%d" % h, name="out_ps%d" % h) for h in range(2)]
-
-        def second_stage_pass(w, h, x_codes, x_scales, start, stop):
-            cols = slice(h * HALF, (h + 1) * HALF)
+        def second_stage_pass(w, piece, x_codes, x_scales, start, stop):
+            cols = slice(*PIECES[piece])
             nc.tensor.matmul_mx(
-                out=out_ps[h][:],
+                out=out_ps[piece][:],
                 lhsT=x_codes[:].bitcast(FP8X4),
                 lhsT_scale=x_scales[:],
                 rhs=w["codes"][:, cols].bitcast(FP8X4),
@@ -216,6 +218,13 @@ def tile_compositionalkoopmanoperators_pa_s_kernel(tc, rel_enc, obj, rp_w, rp_b,
                 start=start,
                 stop=stop,
             )
+
+        def open_piece(piece, tag):
+            first, last = PIECES[piece]
+            out_ps.append(psum.tile([P, last - first], F32, tag=tag, name="out_ps%d" % piece))
+            second_stage_pass(p_obj, piece, obj_codes, obj_scales, True, False)
+
+        out_ps = []
 
         nc.vector.quantize_mx(out=send_codes[:].bitcast(FP8X4), scales=send_scales[:], in_=send_grouped[:])
         quantise_half(w_rel, LOW)
@@ -234,13 +243,28 @@ def tile_compositionalkoopmanoperators_pa_s_kernel(tc, rel_enc, obj, rp_w, rp_b,
         receiver_passes(HIGH)
         quantise_half(w_send, LOW)
         sender_passes(LOW)
+        regroup_on_vector(p_obj, VECTOR_COLS_P_OBJ)
         quantise_half(w_send, HIGH)
         sender_passes(HIGH)
-        regroup_on_vector(p_obj, VECTOR_COLS_P_OBJ)
         regroup_on_scalar(p_obj, VECTOR_COLS_P_OBJ)
-        regroup_on_vector(p_agg, VECTOR_COLS_P_AGG)
+        high_rows = psum.tile([P, PACK, HALF], BF16, tag="obj_scalar", name="high_rows")
+        for t in range(PACK):
+            nc.tensor.matmul(
+                out=high_rows[:, t, :], lhsT=ident_bf16[:], rhs=p_agg["raw"][:, t, HALF:NF], start=True, stop=True
+            )
         quantise_half(p_obj, LOW)
-        second_stage_pass(p_obj, LOW, obj_codes, obj_scales, True, False)
+        open_piece(0, "half0")
+        stay_warm = psum.tile([P, RELS], F32, tag="obj_vector", name="stay_warm")
+        for repeat in range(STAY_WARM_PASSES):
+            nc.tensor.matmul_mx(
+                out=stay_warm[:],
+                lhsT=obj_codes[:].bitcast(FP8X4),
+                lhsT_scale=obj_scales[:],
+                rhs=rel_codes[:].bitcast(FP8X4),
+                rhs_scale=rel_scales[:],
+                start=True,
+                stop=True,
+            )
 
         eff = [keep.tile([P, 2 * ROWS], F32, name="eff%d" % m) for m in range(PACK)]
         pair = [keep.tile([P, 2, ROWS], F32, name="pair%d" % m) for m in range(PACK)]
@@ -269,12 +293,14 @@ def tile_compositionalkoopmanoperators_pa_s_kernel(tc, rel_enc, obj, rp_w, rp_b,
                     op1=ADD,
                 )
 
-        regroup_on_scalar(p_agg, VECTOR_COLS_P_AGG)
+        regroup(nc.scalar.copy, p_agg["grouped"], p_agg["raw"], 0, HALF)
+        nc.scalar.copy(out=p_agg["grouped"][:, HALF:NF, :], in_=high_rows[:].rearrange("p t n -> p n t"))
         agg_grouped = keep.tile([P, ROWS, PACK], BF16, align_bytes=64)
         agg_codes = keep.tile([P, ROWS], U32, align_bytes=64)
         agg_scales = keep.tile([P, ROWS], U8, align_bytes=64)
         quantise_half(p_obj, HIGH)
-        second_stage_pass(p_obj, HIGH, obj_codes, obj_scales, True, False)
+        open_piece(1, "half1")
+        open_piece(2, "acc0")
         regroup(nc.vector.tensor_copy, agg_grouped, agg_planes, 0, ROWS)
         quantise_half(p_agg, LOW)
         nc.vector.quantize_mx(
@@ -284,9 +310,9 @@ def tile_compositionalkoopmanoperators_pa_s_kernel(tc, rel_enc, obj, rp_w, rp_b,
 
         out_rows = out.rearrange("b i f -> (b i) f")
         result = keep.tile([P, NF], F32)
-        for h in range(2):
-            cols = slice(h * HALF, (h + 1) * HALF)
-            second_stage_pass(p_agg, h, agg_codes, agg_scales, False, True)
-            nc.vector.tensor_add(out=result[:, cols], in0=out_ps[h][:], in1=pp_bias[:, cols])
+        for piece in range(len(PIECES)):
+            cols = slice(*PIECES[piece])
+            second_stage_pass(p_agg, piece, agg_codes, agg_scales, False, True)
+            nc.vector.tensor_add(out=result[:, cols], in0=out_ps[piece][:], in1=pp_bias[:, cols])
             nc.scalar.activation(out=result[:, cols], in_=result[:, cols], func=RELU)
             nc.sync.dma_start(out=out_rows[:, cols], in_=result[:, cols])

from contextlib import ExitStack

import concourse.mybir as mybir
from concourse.masks import make_identity

F32 = mybir.dt.float32
BF16 = mybir.dt.bfloat16
U32 = mybir.dt.uint32
U8 = mybir.dt.uint8
FP8X4 = mybir.dt.float8_e4m3fn_x4
RELU = mybir.ActivationFunctionType.Relu
ADD = mybir.AluOpType.add
MAX = mybir.AluOpType.max

P = 128
PACK = 4
NF = 512
BATCH = 32
NPART = 4
ROWS = BATCH * NPART
RELS = ROWS * NPART
HALF = NF // 2
LOW, HIGH = 0, 1
PIECES = ((0, 256), (256, 384), (384, 512))
RUN = 4

VECTOR_COLS_W_REL = 320
VECTOR_COLS_STAGE1 = 256
VECTOR_COLS_P_OBJ = 256

WARM_PASSES = 8
STAY_WARM_PASSES = 4

FLOPS = 2 * NF * NF * (RELS + 4 * ROWS)


def tile_compositionalkoopmanoperators_pa_s_kernel(tc, rel_enc, obj, rp_w, rp_b, pp_w, pp_b, out):
    nc = tc.nc
    with ExitStack() as ctx:
        ctx.enter_context(tc.manual_schedule())
        keep = ctx.enter_context(tc.tile_pool(name="keep", bufs=1))
        psum = ctx.enter_context(tc.psum_pool(name="psum", bufs=1))

        obj_sb = keep.tile([P, NF], BF16)
        nc.sync.dma_start(out=obj_sb[:], in_=obj.rearrange("b i f -> (b i) f"))
        def weight_tiles(name):
            return {
                "raw": keep.tile([P, PACK, NF], BF16, name=name + "_raw"),
                "grouped": keep.tile([P, NF, PACK], BF16, name=name + "_grouped", align_bytes=64),
                "codes": keep.tile([P, NF], U32, name=name + "_codes", align_bytes=64),
                "scales": keep.tile([P, NF], U8, name=name + "_scales", align_bytes=64),
            }

        def load_pair_order(name, rows):
            w = weight_tiles(name)
            nc.sync.dma_start(
                out=w["raw"][:].rearrange("p (u e) n -> p u (e n)", u=2),
                in_=rows.rearrange("(u p e) n -> p u (e n)", u=2, p=P, e=2),
            )
            return w

        def load_plane_order(name, rows):
            w = weight_tiles(name)
            nc.sync.dma_start(out=w["raw"][:], in_=rows.rearrange("(t p) n -> p t n", t=PACK, p=P))
            return w

        w_rel = load_pair_order("w_rel", rp_w[0:NF, :])
        rel_rows = rel_enc.rearrange("b i (h jj) f -> h (b i) (jj f)", h=2)
        rel_sb = []
        for h in range(2):
            rel_half = keep.tile([P, 2 * NF], BF16, name="rel_sb%d" % h)
            nc.sync.dma_start(out=rel_half[:], in_=rel_rows[h])
            rel_sb.append(rel_half)

        w_recv = load_pair_order("w_recv", rp_w[NF : 2 * NF, :])
        w_send = load_pair_order("w_send", rp_w[2 * NF : 3 * NF, :])
        p_obj = load_pair_order("p_obj", pp_w[0:NF, :])
        rp_bias = keep.tile([P, PACK], BF16)
        with nc.allow_non_contiguous_dma(reason="512 bias values, one element a piece"):
            nc.sync.dma_start(out=rp_bias[:], in_=rp_b.rearrange("(m p) -> p m", m=PACK, p=P))
        p_agg = load_plane_order("p_agg", pp_w[NF : 2 * NF, :])

        pp_bias = keep.tile([P, NF], BF16)
        nc.sync.dma_start(out=pp_bias[:], in_=pp_b.partition_broadcast(P))

        ident = keep.tile([P, P], F32)
        make_identity(nc, ident[:])
        ident_bf16 = keep.tile([P, P], BF16)
        make_identity(nc, ident_bf16[:])

        minus_bias = keep.tile([P, PACK], F32)
        nc.gpsimd.tensor_scalar_mul(out=minus_bias[:], in0=rp_bias[:], scalar1=-1.0)
        twice_bias = keep.tile([P, PACK], F32)
        nc.gpsimd.tensor_scalar_mul(out=twice_bias[:], in0=rp_bias[:], scalar1=2.0)

        def regroup(copy, grouped, raw, first, last):
            copy(
                out=grouped[:, first:last, :].rearrange("p (c i) t -> p c t i", i=RUN),
                in_=raw[:, :, first:last].rearrange("p t (c i) -> p c t i", i=RUN),
            )

        def regroup_on_vector(w, vector_cols):
            regroup(nc.vector.tensor_copy, w["grouped"], w["raw"], 0, vector_cols)

        def regroup_on_scalar(w, vector_cols):
            regroup(nc.scalar.copy, w["grouped"], w["raw"], vector_cols, NF)

        def quantise_half(w, h):
            cols = slice(h * HALF, (h + 1) * HALF)
            nc.vector.quantize_mx(
                out=w["codes"][:, cols].bitcast(FP8X4),
                scales=w["scales"][:, cols],
                in_=w["grouped"][:, cols, :].rearrange("p n t -> p (n t)"),
            )

        obj_words = obj_sb[:].bitcast(F32)
        obj_t = []
        for reader in ("vector", "scalar"):
            bank = psum.tile([P, 2, ROWS], F32, tag="obj_" + reader, name="obj_t_" + reader)
            for u in range(2):
                nc.tensor.transpose(bank[:, u, :], obj_words[:, u * P : (u + 1) * P], ident[:])
            obj_t.append(bank)
        rel_t = []
        for h in range(2):
            rel_words = rel_sb[h][:].bitcast(F32)
            bank = psum.tile([P, 2, 2, ROWS], F32, tag="half%d" % h, name="rel_t%d" % h)
            for jj in range(2):
                for u in range(2):
                    first = (jj * 2 + u) * P
                    nc.tensor.transpose(bank[:, jj, u, :], rel_words[:, first : first + P], ident[:])
            rel_t.append(bank)

        obj_grouped = keep.tile([P, ROWS * PACK], BF16, align_bytes=64)
        nc.vector.tensor_copy(
            out=obj_grouped[:].bitcast(F32).rearrange("p (r u) -> p r u", u=2),
            in_=obj_t[0][:].rearrange("p u r -> p r u"),
        )
        obj_codes = keep.tile([P, ROWS], U32, align_bytes=64)
        obj_scales = keep.tile([P, ROWS], U8, align_bytes=64)
        send_grouped = keep.tile([P, RELS * PACK], BF16, align_bytes=64)
        send_view = send_grouped[:].bitcast(F32).rearrange("p (j b i u) -> p j b i u", j=NPART, b=BATCH, i=NPART)
        for j in range(NPART):
            copy, bank = (nc.vector.tensor_copy, obj_t[0]) if j == 0 else (nc.scalar.copy, obj_t[1])
            obj_by_sender = bank[:].rearrange("p u (b j) -> p j b u", j=NPART)
            copy(
                out=send_view[:, j],
                in_=obj_by_sender[:, j].unsqueeze(2).to_broadcast([P, BATCH, NPART, 2]),
            )
        nc.vector.quantize_mx(out=obj_codes[:].bitcast(FP8X4), scales=obj_scales[:], in_=obj_grouped[:])
        regroup_on_vector(w_rel, VECTOR_COLS_W_REL)
        regroup_on_scalar(w_rel, VECTOR_COLS_W_REL)
        rel_grouped = keep.tile([P, RELS * PACK], BF16, align_bytes=64)
        rel_view = rel_grouped[:].bitcast(F32).rearrange("p (h jj r u) -> p h jj r u", h=2, jj=2, u=2)
        for h in range(2):
            nc.scalar.copy(out=rel_view[:, h], in_=rel_t[h][:].rearrange("p jj u r -> p jj r u"))
        rel_codes = keep.tile([P, RELS], U32, align_bytes=64)
        rel_scales = keep.tile([P, RELS], U8, align_bytes=64)
        send_codes = keep.tile([P, RELS], U32, align_bytes=64)
        send_scales = keep.tile([P, RELS], U8, align_bytes=64)

        warm = psum.tile([P, ROWS], F32, tag="obj_vector", name="warm")
        for repeat in range(WARM_PASSES):
            nc.tensor.matmul_mx(
                out=warm[:],
                lhsT=obj_codes[:].bitcast(FP8X4),
                lhsT_scale=obj_scales[:],
                rhs=obj_codes[:].bitcast(FP8X4),
                rhs_scale=obj_scales[:],
                start=True,
                stop=True,
            )

        acc = [psum.tile([P, RELS], F32, tag="acc%d" % m, name="acc%d" % m) for m in range(PACK)]

        def first_stage_pass(w, m, out_cols, x_codes, x_scales, start, stop):
            cols = slice(m * P, (m + 1) * P)
            nc.tensor.matmul_mx(
                out=out_cols,
                lhsT=w["codes"][:, cols].bitcast(FP8X4),
                lhsT_scale=w["scales"][:, cols],
                rhs=x_codes.bitcast(FP8X4),
                rhs_scale=x_scales,
                start=start,
                stop=stop,
            )

        def quantise_relations(h):
            cols = slice(h * RELS // 2, (h + 1) * RELS // 2)
            nc.vector.quantize_mx(
                out=rel_codes[:, cols].bitcast(FP8X4),
                scales=rel_scales[:, cols],
                in_=rel_grouped[:, h * RELS // 2 * PACK : (h + 1) * RELS // 2 * PACK],
            )

        def relation_passes(h):
            cols = slice(h * RELS // 2, (h + 1) * RELS // 2)
            for m in range(PACK):
                first_stage_pass(w_rel, m, acc[m][:, cols], rel_codes[:, cols], rel_scales[:, cols], h == 0, False)

        def receiver_passes(h):
            for m in (2 * h, 2 * h + 1):
                by_sender = acc[m][:].rearrange("p (j r) -> p j r", j=NPART)
                for j in range(NPART):
                    first_stage_pass(w_recv, m, by_sender[:, j], obj_codes[:], obj_scales[:], False, False)

        def sender_passes(h):
            for m in (2 * h, 2 * h + 1):
                first_stage_pass(w_send, m, acc[m][:], send_codes[:], send_scales[:], False, True)

        def second_stage_pass(w, piece, x_codes, x_scales, start, stop):
            cols = slice(*PIECES[piece])
            nc.tensor.matmul_mx(
                out=out_ps[piece][:],
                lhsT=x_codes[:].bitcast(FP8X4),
                lhsT_scale=x_scales[:],
                rhs=w["codes"][:, cols].bitcast(FP8X4),
                rhs_scale=w["scales"][:, cols],
                start=start,
                stop=stop,
            )

        def open_piece(piece, tag):
            first, last = PIECES[piece]
            out_ps.append(psum.tile([P, last - first], F32, tag=tag, name="out_ps%d" % piece))
            second_stage_pass(p_obj, piece, obj_codes, obj_scales, True, False)

        out_ps = []

        nc.vector.quantize_mx(out=send_codes[:].bitcast(FP8X4), scales=send_scales[:], in_=send_grouped[:])
        quantise_half(w_rel, LOW)
        quantise_half(w_rel, HIGH)
        quantise_relations(0)
        relation_passes(0)
        regroup_on_vector(w_recv, VECTOR_COLS_STAGE1)
        regroup_on_scalar(w_recv, VECTOR_COLS_STAGE1)
        quantise_relations(1)
        relation_passes(1)
        quantise_half(w_recv, LOW)
        receiver_passes(LOW)
        regroup_on_vector(w_send, VECTOR_COLS_STAGE1)
        regroup_on_scalar(w_send, VECTOR_COLS_STAGE1)
        quantise_half(w_recv, HIGH)
        receiver_passes(HIGH)
        quantise_half(w_send, LOW)
        sender_passes(LOW)
        regroup_on_vector(p_obj, VECTOR_COLS_P_OBJ)
        quantise_half(w_send, HIGH)
        sender_passes(HIGH)
        regroup_on_scalar(p_obj, VECTOR_COLS_P_OBJ)
        high_rows = psum.tile([P, PACK, HALF], BF16, tag="obj_scalar", name="high_rows")
        for t in range(PACK):
            nc.tensor.matmul(
                out=high_rows[:, t, :], lhsT=ident_bf16[:], rhs=p_agg["raw"][:, t, HALF:NF], start=True, stop=True
            )
        quantise_half(p_obj, LOW)
        open_piece(0, "half0")
        stay_warm = psum.tile([P, RELS], F32, tag="obj_vector", name="stay_warm")
        for repeat in range(STAY_WARM_PASSES):
            nc.tensor.matmul_mx(
                out=stay_warm[:],
                lhsT=obj_codes[:].bitcast(FP8X4),
                lhsT_scale=obj_scales[:],
                rhs=rel_codes[:].bitcast(FP8X4),
                rhs_scale=rel_scales[:],
                start=True,
                stop=True,
            )

        eff = [keep.tile([P, 2 * ROWS], F32, name="eff%d" % m) for m in range(PACK)]
        pair = [keep.tile([P, 2, ROWS], F32, name="pair%d" % m) for m in range(PACK)]
        agg_planes = keep.tile([P, PACK, ROWS], BF16)
        for m in range(PACK):
            nc.scalar.activation(
                out=eff[m][:], in_=acc[m][:, 0 : 2 * ROWS], func=RELU, bias=rp_bias[:, m : m + 1], scale=1.0
            )
        for h in range(2):
            for m in (2 * h, 2 * h + 1):
                nc.vector.scalar_tensor_tensor(
                    out=pair[m][:].rearrange("p j r -> p (j r)"),
                    in0=acc[m][:, 2 * ROWS : RELS],
                    scalar=minus_bias[:, m : m + 1],
                    in1=eff[m][:],
                    op0=MAX,
                    op1=ADD,
                )
            for m in (2 * h, 2 * h + 1):
                nc.vector.scalar_tensor_tensor(
                    out=agg_planes[:, m, :],
                    in0=pair[m][:, 0, :],
                    scalar=twice_bias[:, m : m + 1],
                    in1=pair[m][:, 1, :],
                    op0=ADD,
                    op1=ADD,
                )

        regroup(nc.scalar.copy, p_agg["grouped"], p_agg["raw"], 0, HALF)
        nc.scalar.copy(out=p_agg["grouped"][:, HALF:NF, :], in_=high_rows[:].rearrange("p t n -> p n t"))
        agg_grouped = keep.tile([P, ROWS, PACK], BF16, align_bytes=64)
        agg_codes = keep.tile([P, ROWS], U32, align_bytes=64)
        agg_scales = keep.tile([P, ROWS], U8, align_bytes=64)
        quantise_half(p_obj, HIGH)
        open_piece(1, "half1")
        open_piece(2, "acc0")
        regroup(nc.vector.tensor_copy, agg_grouped, agg_planes, 0, ROWS)
        quantise_half(p_agg, LOW)
        nc.vector.quantize_mx(
            out=agg_codes[:].bitcast(FP8X4), scales=agg_scales[:], in_=agg_grouped[:].rearrange("p r t -> p (r t)")
        )
        quantise_half(p_agg, HIGH)

        out_rows = out.rearrange("b i f -> (b i) f")
        result = keep.tile([P, NF], F32)
        for piece in range(len(PIECES)):
            cols = slice(*PIECES[piece])
            second_stage_pass(p_agg, piece, agg_codes, agg_scales, False, True)
            nc.vector.tensor_add(out=result[:, cols], in0=out_ps[piece][:], in1=pp_bias[:, cols])
            nc.scalar.activation(out=result[:, cols], in_=result[:, cols], func=RELU)
            nc.sync.dma_start(out=out_rows[:, cols], in_=result[:, cols])
